import numpy as np
import ml_dtypes


def mxq(x, axis, fmt="e4m3"):
    dtype, down = {"e4m3": (ml_dtypes.float8_e4m3fn, 7), "e5m2": (ml_dtypes.float8_e5m2, 14)}[fmt]
    v = np.moveaxis(np.asarray(x, np.float32).astype(ml_dtypes.bfloat16).astype(np.float64), axis, -1)
    blocks = v.reshape(v.shape[:-1] + (-1, 32))
    amax = np.abs(blocks).max(-1, keepdims=True)
    byte = np.maximum(np.where(amax > 0, np.frexp(amax)[1] - 1 + 127, 0) - down, 1)
    scale = np.exp2(byte - 127.0)
    codes = (blocks / scale).astype(np.float32).astype(dtype).astype(np.float64)
    return np.moveaxis((codes * scale).reshape(v.shape), -1, axis)


WIDE = False


def mx_kscale(k):
    if not WIDE:
        return np.ones(k)
    levels = np.array([10, -10, 5, -5, 0])
    a = np.random.permutation(np.resize(levels, k // 512 * 4)).reshape(k // 512, 4)
    idx = np.arange(k)
    return np.exp2(a[idx // 512, idx % 128 // 32])


BF16 = ml_dtypes.bfloat16


def bf(x):
    return np.asarray(x, np.float32).astype(BF16)


def f64(x):
    return np.asarray(x).astype(np.float64)


E2M1 = np.array([0.0, 0.5, 1.0, 1.5, 2.0, 3.0, 4.0, 6.0, -0.0, -0.5, -1.0, -1.5, -2.0, -3.0, -4.0, -6.0])


def pack_weight(w, fmt):
    k, n = w.shape
    w = f64(bf(w)).reshape(k // 32, 32, n)
    amax = np.abs(w).max(1)
    if fmt == "e4m3":
        byte = np.frexp(amax)[1] - 1 + 127 - 7
    else:
        mant, ex = np.frexp(amax / 6.0)
        byte = np.where(mant > 0.5, ex, ex - 1) + 127
    byte = np.clip(np.where(amax > 0, byte, 1), 1, 254)
    scaled = (w * np.exp2(127.0 - byte)[:, None, :]).reshape(k, n).astype(np.float32)
    by_word = np.ascontiguousarray(scaled.reshape(k // 512, 128, 4, n).transpose(0, 1, 3, 2))
    if fmt == "e4m3":
        words = by_word.astype(ml_dtypes.float8_e4m3fn).view(np.uint8)
    else:
        c = by_word.astype(ml_dtypes.float4_e2m1fn).view(np.uint8) & 0xF
        words = c[..., 0::2] | (c[..., 1::2] << 4)
    return np.ascontiguousarray(words), np.ascontiguousarray(byte.astype(np.uint8).reshape(k // 512, 16, n))


def unpack_weight(words, scales, fmt):
    g, p, n, _ = words.shape
    if fmt == "e4m3":
        vals = np.ascontiguousarray(words).view(ml_dtypes.float8_e4m3fn).astype(np.float64)
    else:
        nib = np.empty((g, p, n, 4), np.uint8)
        nib[..., 0::2] = words & 0xF
        nib[..., 1::2] = words >> 4
        vals = E2M1[nib]
    vals = vals * np.repeat(np.exp2(scales.astype(np.float64) - 127.0), 8, axis=1)[..., None]
    return vals.transpose(0, 1, 3, 2).reshape(g * 512, n)


B, CB, CD, H, W = 2, 2, 3072, 8, 8
C = CB * CD


def erf(z):
    z = np.clip(z, -6.0, 6.0)
    z2 = 2.0 * z * z
    term = z.copy()
    tot = z.copy()
    for n in range(1, 101):
        term *= z2
        term /= 2 * n + 1
        tot += term
    return 2.0 / np.sqrt(np.pi) * np.exp(-z * z) * tot


def gelu_erf(v):
    return 0.5 * v * (1.0 + erf(v / np.sqrt(2.0)))


def setup_inputs():
    s = mx_kscale(CD)
    s = s / s.max()
    sc = np.tile(s, CB)
    x = bf(np.random.standard_normal((B, C, H, W)) * sc[None, :, None, None])
    stack = np.random.standard_normal((CB, CD, CD)) / np.sqrt(CD) / s[None, :, None]
    words, scales = pack_weight(stack.reshape(-1, CD), "e4m3")
    return {"x": x, "wc_words": words, "wc_scales": scales}


def reference(x, wc_words, wc_scales):
    x = f64(x)
    xr = np.transpose(x, (0, 2, 3, 1)).reshape(B, H, W, CB, CD)
    xb = xr.transpose(3, 0, 1, 2, 4).reshape(CB, B * H * W, CD)
    out = mxq(xb, 2, "e4m3") @ unpack_weight(wc_words, wc_scales, "e4m3").reshape(CB, CD, CD)
    out = out.reshape(CB, B, H, W, CD).transpose(1, 2, 3, 0, 4)
    out = out.reshape(B, H, W, C).transpose(0, 3, 1, 2)
    return gelu_erf(x + out)

@@ -1,0 +1,134 @@
+from contextlib import ExitStack
+
+import concourse.mybir as mybir
+from concourse.masks import make_identity
+
+BF16 = mybir.dt.bfloat16
+F32 = mybir.dt.float32
+I32 = mybir.dt.int32
+U32 = mybir.dt.uint32
+U8 = mybir.dt.uint8
+FP8X4 = mybir.dt.float8_e4m3fn_x4
+
+P = 128
+PACK = 4
+GROUP = P * PACK
+BATCH = 2
+PIXELS = 64
+TOKENS = BATCH * PIXELS
+BLOCKS = 2
+BLOCK_CH = 3072
+STEPS = BLOCK_CH // GROUP
+GROUPS = BLOCKS * STEPS
+PLANES_PER_TILE = 4
+PLANE_TILES = GROUPS // PLANES_PER_TILE
+QUADRANTS = 4
+QUANT_GROUPS = 4
+
+FLOPS = 2 * TOKENS * BLOCKS * BLOCK_CH * BLOCK_CH
+
+
+def tile_spectralchannelmixing_w_e_kernel(tc, x, wc_words, wc_scales, out):
+    nc = tc.nc
+
+    x_view = x.rearrange("b (g p t) h w -> b p g (t h w)", p=P, t=PACK)
+    out_view = out.rearrange("b (g p t) h w -> g p b (t h w)", p=P, t=PACK)
+
+    with ExitStack() as ctx:
+        keep = ctx.enter_context(tc.tile_pool(name="keep", bufs=1))
+        stage = ctx.enter_context(tc.tile_pool(name="stage", bufs=2))
+        mixed_pool = ctx.enter_context(tc.tile_pool(name="mixed", bufs=STEPS))
+        acc_pool = ctx.enter_context(tc.psum_pool(name="acc", bufs=STEPS))
+        turned_pool = ctx.enter_context(tc.psum_pool(name="turned", bufs=2))
+        ctx.enter_context(tc.manual_schedule())
+
+        x_sb = keep.tile([P, GROUPS, BATCH, PACK * PIXELS], BF16)
+        for b in range(BATCH):
+            nc.sync.dma_start(out=x_sb[:, :, b, :], in_=x_view[b])
+
+        w_planes = keep.tile([P, PLANE_TILES, BLOCK_CH], U8, align_bytes=64)
+        nc.vector.memset(w_planes[:].bitcast(I32), 0)
+        for j in range(PLANE_TILES):
+            for q in range(QUADRANTS):
+                nc.sync.dma_start(
+                    out=w_planes[32 * q : 32 * q + 16, j, :].bitcast(I32),
+                    in_=wc_scales[
+                        PLANES_PER_TILE * j : PLANES_PER_TILE * (j + 1), 4 * q : 4 * q + 4, :
+                    ].bitcast(I32),
+                )
+
+        w_words = []
+        for g in range(GROUPS):
+            words = keep.tile([P, BLOCK_CH], I32, name="w_words%d" % g, align_bytes=64)
+            nc.sync.dma_start(
+                out=words[:], in_=wc_words[g].rearrange("p n t -> p (n t)").bitcast(I32)
+            )
+            w_words.append(words)
+
+        ident = keep.tile([P, P], F32)
+        make_identity(nc, ident[:])
+
+        x_codes = keep.tile([P, GROUPS * TOKENS], U32, align_bytes=64)
+        x_scales = keep.tile([P, GROUPS * TOKENS], U8, align_bytes=64)
+        for g0 in range(0, GROUPS, QUANT_GROUPS):
+            grouped = stage.tile([P, QUANT_GROUPS * TOKENS, PACK], BF16, align_bytes=64)
+            nc.vector.tensor_copy(
+                out=grouped[:].rearrange("p (u s) t -> p u s t", s=PIXELS),
+                in_=x_sb[:, g0 : g0 + QUANT_GROUPS, :, :].rearrange(
+                    "p g b (t s) -> p (g b) s t", t=PACK
+                ),
+            )
+            cols = slice(g0 * TOKENS, (g0 + QUANT_GROUPS) * TOKENS)
+            nc.vector.quantize_mx(
+                out=x_codes[:, cols].bitcast(FP8X4),
+                scales=x_scales[:, cols],
+                in_=grouped[:].rearrange("p m t -> p (m t)"),
+            )
+
+        mixed_of = {}
+
+        def finish(g):
+            mixed = mixed_of[g]
+            turned = turned_pool.tile([P, PACK, TOKENS], F32)
+            for t in range(PACK):
+                nc.tensor.transpose(turned[:, t, :], mixed[:, t, :], ident[:])
+            result = keep.tile([P, BATCH, PACK, PIXELS], F32, name="result%d" % g)
+            nc.vector.tensor_tensor(
+                out=result[:],
+                in0=turned[:].rearrange("p t (b s) -> p b t s", b=BATCH),
+                in1=x_sb[:, g, :, :].rearrange("p b (t s) -> p b t s", t=PACK),
+                op=mybir.AluOpType.add,
+            )
+            nc.scalar.activation(
+                out=result[:], in_=result[:], func=mybir.ActivationFunctionType.Gelu
+            )
+            nc.sync.dma_start(out=out_view[g], in_=result[:].rearrange("p b t s -> p b (t s)"))
+
+        for block in range(BLOCKS):
+            acc = [acc_pool.tile([P, GROUP], F32, name="acc%d" % n, tag="acc") for n in range(STEPS)]
+            for step in range(STEPS):
+                g = block * STEPS + step
+                if block > 0:
+                    finish(g - STEPS)
+                offset = 4 * (g % PLANES_PER_TILE)
+                for n in range(STEPS):
+                    cols = slice(n * GROUP, (n + 1) * GROUP)
+                    nc.tensor.matmul_mx(
+                        out=acc[n][:],
+                        lhsT=x_codes[:, g * TOKENS : (g + 1) * TOKENS].bitcast(FP8X4),
+                        lhsT_scale=x_scales[:, g * TOKENS : (g + 1) * TOKENS],
+                        rhs=w_words[g][:, cols].bitcast(FP8X4),
+                        rhs_scale=w_planes[offset:P, g // PLANES_PER_TILE, cols],
+                        start=(step == 0),
+                        stop=(step == STEPS - 1),
+                    )
+            for n in range(STEPS):
+                mixed = mixed_pool.tile([P, PACK, P], F32)
+                sorted_bank = acc[n][:].rearrange("m (c t) -> m t c", t=PACK)
+                if n % 2 == 0:
+                    nc.scalar.copy(out=mixed[:], in_=sorted_bank)
+                else:
+                    nc.vector.tensor_copy(out=mixed[:], in_=sorted_bank)
+                mixed_of[block * STEPS + n] = mixed
+        for n in range(STEPS):
+            finish((BLOCKS - 1) * STEPS + n)

@@ -50,11 +50,11 @@ def tile_spectralchannelmixing_w_e_kernel(tc, x, wc_words, wc_scales, out):
         nc.vector.memset(w_planes[:].bitcast(I32), 0)
         for j in range(PLANE_TILES):
             for q in range(QUADRANTS):
-                nc.sync.dma_start(
-                    out=w_planes[32 * q : 32 * q + 16, j, :].bitcast(I32),
+                nc.gpsimd.dma_start(
+                    out=w_planes[32 * q : 32 * q + 16, j, :].bitcast(F32),
                     in_=wc_scales[
                         PLANES_PER_TILE * j : PLANES_PER_TILE * (j + 1), 4 * q : 4 * q + 4, :
-                    ].bitcast(I32),
+                    ].bitcast(F32),
                 )
 
         w_words = []

@@ -37,7 +37,7 @@ def tile_spectralchannelmixing_w_e_kernel(tc, x, wc_words, wc_scales, out):
     with ExitStack() as ctx:
         keep = ctx.enter_context(tc.tile_pool(name="keep", bufs=1))
         stage = ctx.enter_context(tc.tile_pool(name="stage", bufs=2))
-        mixed_pool = ctx.enter_context(tc.tile_pool(name="mixed", bufs=STEPS))
+        mixed_pool = ctx.enter_context(tc.tile_pool(name="mixed", bufs=3))
         acc_pool = ctx.enter_context(tc.psum_pool(name="acc", bufs=STEPS))
         turned_pool = ctx.enter_context(tc.psum_pool(name="turned", bufs=2))
         ctx.enter_context(tc.manual_schedule())
@@ -50,19 +50,23 @@ def tile_spectralchannelmixing_w_e_kernel(tc, x, wc_words, wc_scales, out):
         nc.vector.memset(w_planes[:].bitcast(I32), 0)
         for j in range(PLANE_TILES):
             for q in range(QUADRANTS):
-                nc.gpsimd.dma_start(
-                    out=w_planes[32 * q : 32 * q + 16, j, :].bitcast(F32),
+                nc.sync.dma_start(
+                    out=w_planes[32 * q : 32 * q + 16, j, :].bitcast(I32),
                     in_=wc_scales[
                         PLANES_PER_TILE * j : PLANES_PER_TILE * (j + 1), 4 * q : 4 * q + 4, :
-                    ].bitcast(F32),
+                    ].bitcast(I32),
                 )
 
         w_words = []
         for g in range(GROUPS):
             words = keep.tile([P, BLOCK_CH], I32, name="w_words%d" % g, align_bytes=64)
-            nc.sync.dma_start(
-                out=words[:], in_=wc_words[g].rearrange("p n t -> p (n t)").bitcast(I32)
-            )
+            source = wc_words[g].rearrange("p n t -> p (n t)").bitcast(I32)
+            if g < GROUPS - 1:
+                nc.sync.dma_start(out=words[:], in_=source)
+            else:
+                for n in range(STEPS):
+                    cols = slice(n * GROUP, (n + 1) * GROUP)
+                    nc.sync.dma_start(out=words[:, cols], in_=source[:, cols])
             w_words.append(words)
 
         ident = keep.tile([P, P], F32)
@@ -104,31 +108,35 @@ def tile_spectralchannelmixing_w_e_kernel(tc, x, wc_words, wc_scales, out):
             )
             nc.sync.dma_start(out=out_view[g], in_=result[:].rearrange("p b t s -> p b (t s)"))
 
+        def multiply(g, acc, n):
+            step = g % STEPS
+            offset = 4 * (g % PLANES_PER_TILE)
+            cols = slice(n * GROUP, (n + 1) * GROUP)
+            nc.tensor.matmul_mx(
+                out=acc[n][:],
+                lhsT=x_codes[:, g * TOKENS : (g + 1) * TOKENS].bitcast(FP8X4),
+                lhsT_scale=x_scales[:, g * TOKENS : (g + 1) * TOKENS],
+                rhs=w_words[g][:, cols].bitcast(FP8X4),
+                rhs_scale=w_planes[offset:P, g // PLANES_PER_TILE, cols],
+                start=(step == 0),
+                stop=(step == STEPS - 1),
+            )
+
         for block in range(BLOCKS):
+            first = block * STEPS
             acc = [acc_pool.tile([P, GROUP], F32, name="acc%d" % n, tag="acc") for n in range(STEPS)]
-            for step in range(STEPS):
-                g = block * STEPS + step
-                if block > 0:
-                    finish(g - STEPS)
-                offset = 4 * (g % PLANES_PER_TILE)
+            for step in range(STEPS - 1):
                 for n in range(STEPS):
-                    cols = slice(n * GROUP, (n + 1) * GROUP)
-                    nc.tensor.matmul_mx(
-                        out=acc[n][:],
-                        lhsT=x_codes[:, g * TOKENS : (g + 1) * TOKENS].bitcast(FP8X4),
-                        lhsT_scale=x_scales[:, g * TOKENS : (g + 1) * TOKENS],
-                        rhs=w_words[g][:, cols].bitcast(FP8X4),
-                        rhs_scale=w_planes[offset:P, g // PLANES_PER_TILE, cols],
-                        start=(step == 0),
-                        stop=(step == STEPS - 1),
-                    )
+                    multiply(first + step, acc, n)
             for n in range(STEPS):
+                multiply(first + STEPS - 1, acc, n)
                 mixed = mixed_pool.tile([P, PACK, P], F32)
                 sorted_bank = acc[n][:].rearrange("m (c t) -> m t c", t=PACK)
                 if n % 2 == 0:
                     nc.scalar.copy(out=mixed[:], in_=sorted_bank)
                 else:
                     nc.vector.tensor_copy(out=mixed[:], in_=sorted_bank)
-                mixed_of[block * STEPS + n] = mixed
-        for n in range(STEPS):
-            finish((BLOCKS - 1) * STEPS + n)
+                mixed_of[first + n] = mixed
+                if n > 0:
+                    finish(first + n - 1)
+            finish(first + STEPS - 1)

from contextlib import ExitStack

import concourse.mybir as mybir
from concourse.masks import make_identity

BF16 = mybir.dt.bfloat16
F32 = mybir.dt.float32
I32 = mybir.dt.int32
U32 = mybir.dt.uint32
U8 = mybir.dt.uint8
FP8X4 = mybir.dt.float8_e4m3fn_x4

P = 128
PACK = 4
GROUP = P * PACK
BATCH = 2
PIXELS = 64
TOKENS = BATCH * PIXELS
BLOCKS = 2
BLOCK_CH = 3072
STEPS = BLOCK_CH // GROUP
GROUPS = BLOCKS * STEPS
PLANES_PER_TILE = 4
PLANE_TILES = GROUPS // PLANES_PER_TILE
QUADRANTS = 4
QUANT_GROUPS = 4

FLOPS = 2 * TOKENS * BLOCKS * BLOCK_CH * BLOCK_CH


def tile_spectralchannelmixing_w_e_kernel(tc, x, wc_words, wc_scales, out):
    nc = tc.nc

    x_view = x.rearrange("b (g p t) h w -> b p g (t h w)", p=P, t=PACK)
    out_view = out.rearrange("b (g p t) h w -> g p b (t h w)", p=P, t=PACK)

    with ExitStack() as ctx:
        keep = ctx.enter_context(tc.tile_pool(name="keep", bufs=1))
        stage = ctx.enter_context(tc.tile_pool(name="stage", bufs=2))
        mixed_pool = ctx.enter_context(tc.tile_pool(name="mixed", bufs=3))
        acc_pool = ctx.enter_context(tc.psum_pool(name="acc", bufs=STEPS))
        turned_pool = ctx.enter_context(tc.psum_pool(name="turned", bufs=2))
        ctx.enter_context(tc.manual_schedule())

        x_sb = keep.tile([P, GROUPS, BATCH, PACK * PIXELS], BF16)
        for b in range(BATCH):
            nc.sync.dma_start(out=x_sb[:, :, b, :], in_=x_view[b])

        w_planes = keep.tile([P, PLANE_TILES, BLOCK_CH], U8, align_bytes=64)
        nc.vector.memset(w_planes[:].bitcast(I32), 0)
        for j in range(PLANE_TILES):
            for q in range(QUADRANTS):
                nc.sync.dma_start(
                    out=w_planes[32 * q : 32 * q + 16, j, :].bitcast(I32),
                    in_=wc_scales[
                        PLANES_PER_TILE * j : PLANES_PER_TILE * (j + 1), 4 * q : 4 * q + 4, :
                    ].bitcast(I32),
                )

        w_words = []
        for g in range(GROUPS):
            words = keep.tile([P, BLOCK_CH], I32, name="w_words%d" % g, align_bytes=64)
            source = wc_words[g].rearrange("p n t -> p (n t)").bitcast(I32)
            if g < GROUPS - 1:
                nc.sync.dma_start(out=words[:], in_=source)
            else:
                for n in range(STEPS):
                    cols = slice(n * GROUP, (n + 1) * GROUP)
                    nc.sync.dma_start(out=words[:, cols], in_=source[:, cols])
            w_words.append(words)

        ident = keep.tile([P, P], F32)
        make_identity(nc, ident[:])

        x_codes = keep.tile([P, GROUPS * TOKENS], U32, align_bytes=64)
        x_scales = keep.tile([P, GROUPS * TOKENS], U8, align_bytes=64)
        for g0 in range(0, GROUPS, QUANT_GROUPS):
            grouped = stage.tile([P, QUANT_GROUPS * TOKENS, PACK], BF16, align_bytes=64)
            nc.vector.tensor_copy(
                out=grouped[:].rearrange("p (u s) t -> p u s t", s=PIXELS),
                in_=x_sb[:, g0 : g0 + QUANT_GROUPS, :, :].rearrange(
                    "p g b (t s) -> p (g b) s t", t=PACK
                ),
            )
            cols = slice(g0 * TOKENS, (g0 + QUANT_GROUPS) * TOKENS)
            nc.vector.quantize_mx(
                out=x_codes[:, cols].bitcast(FP8X4),
                scales=x_scales[:, cols],
                in_=grouped[:].rearrange("p m t -> p (m t)"),
            )

        mixed_of = {}

        def finish(g):
            mixed = mixed_of[g]
            turned = turned_pool.tile([P, PACK, TOKENS], F32)
            for t in range(PACK):
                nc.tensor.transpose(turned[:, t, :], mixed[:, t, :], ident[:])
            result = keep.tile([P, BATCH, PACK, PIXELS], F32, name="result%d" % g)
            nc.vector.tensor_tensor(
                out=result[:],
                in0=turned[:].rearrange("p t (b s) -> p b t s", b=BATCH),
                in1=x_sb[:, g, :, :].rearrange("p b (t s) -> p b t s", t=PACK),
                op=mybir.AluOpType.add,
            )
            nc.scalar.activation(
                out=result[:], in_=result[:], func=mybir.ActivationFunctionType.Gelu
            )
            nc.sync.dma_start(out=out_view[g], in_=result[:].rearrange("p b t s -> p b (t s)"))

        def multiply(g, acc, n):
            step = g % STEPS
            offset = 4 * (g % PLANES_PER_TILE)
            cols = slice(n * GROUP, (n + 1) * GROUP)
            nc.tensor.matmul_mx(
                out=acc[n][:],
                lhsT=x_codes[:, g * TOKENS : (g + 1) * TOKENS].bitcast(FP8X4),
                lhsT_scale=x_scales[:, g * TOKENS : (g + 1) * TOKENS],
                rhs=w_words[g][:, cols].bitcast(FP8X4),
                rhs_scale=w_planes[offset:P, g // PLANES_PER_TILE, cols],
                start=(step == 0),
                stop=(step == STEPS - 1),
            )

        for block in range(BLOCKS):
            first = block * STEPS
            acc = [acc_pool.tile([P, GROUP], F32, name="acc%d" % n, tag="acc") for n in range(STEPS)]
            for step in range(STEPS - 1):
                for n in range(STEPS):
                    multiply(first + step, acc, n)
            for n in range(STEPS):
                multiply(first + STEPS - 1, acc, n)
                mixed = mixed_pool.tile([P, PACK, P], F32)
                sorted_bank = acc[n][:].rearrange("m (c t) -> m t c", t=PACK)
                if n % 2 == 0:
                    nc.scalar.copy(out=mixed[:], in_=sorted_bank)
                else:
                    nc.vector.tensor_copy(out=mixed[:], in_=sorted_bank)
                mixed_of[first + n] = mixed
                if n > 0:
                    finish(first + n - 1)
            finish(first + STEPS - 1)
